import numpy as np
import ml_dtypes


def mxq(x, axis, fmt="e4m3"):
    dtype, down = {"e4m3": (ml_dtypes.float8_e4m3fn, 7), "e5m2": (ml_dtypes.float8_e5m2, 14)}[fmt]
    v = np.moveaxis(np.asarray(x, np.float32).astype(ml_dtypes.bfloat16).astype(np.float64), axis, -1)
    blocks = v.reshape(v.shape[:-1] + (-1, 32))
    amax = np.abs(blocks).max(-1, keepdims=True)
    byte = np.maximum(np.where(amax > 0, np.frexp(amax)[1] - 1 + 127, 0) - down, 1)
    scale = np.exp2(byte - 127.0)
    codes = (blocks / scale).astype(np.float32).astype(dtype).astype(np.float64)
    return np.moveaxis((codes * scale).reshape(v.shape), -1, axis)


WIDE = False


def mx_kscale(k):
    if not WIDE:
        return np.ones(k)
    levels = np.array([10, -10, 5, -5, 0])
    a = np.random.permutation(np.resize(levels, k // 512 * 4)).reshape(k // 512, 4)
    idx = np.arange(k)
    return np.exp2(a[idx // 512, idx % 128 // 32])


BF16 = ml_dtypes.bfloat16


def bf(x):
    return np.asarray(x, np.float32).astype(BF16)


def f64(x):
    return np.asarray(x).astype(np.float64)


B, N, F = 1, 1024, 1024


def setup_inputs():
    s = mx_kscale(F)
    limit = np.sqrt(6.0 / (F + F))
    return {"nodes": bf(np.random.standard_normal((B, N, F)) * s),
            "W": bf(np.random.uniform(-limit, limit, (F, F)) / s[:, None] / s[None, :])}


def reference(nodes, W):
    norm_const = 1.0 / np.sqrt(F)
    nq = mxq(f64(nodes), 2, "e4m3")
    x = nq @ mxq(f64(W), 0, "e4m3")
    prods = mxq(x, 2, "e4m3") @ nq.transpose(0, 2, 1)
    z = prods * norm_const
    e = np.exp(z - z.max(-1, keepdims=True))
    return e / e.sum(-1, keepdims=True)

@@ -1,0 +1,201 @@
+from contextlib import ExitStack
+
+import concourse.mybir as mybir
+from concourse.masks import make_identity
+
+BF16 = mybir.dt.bfloat16
+F32 = mybir.dt.float32
+U32 = mybir.dt.uint32
+U8 = mybir.dt.uint8
+FP8X4 = mybir.dt.float8_e4m3fn_x4
+ACT = mybir.ActivationFunctionType
+ALU = mybir.AluOpType
+AXIS = mybir.AxisListType
+
+P = 128
+PACK = 4
+K_PASS = P * PACK
+NODES = 1024
+FEATURES = 1024
+PASSES = FEATURES // K_PASS
+BLOCKS = NODES // P
+BANK = 512
+HALVES = NODES // BANK
+LOOKAHEAD = 2
+
+FLOPS = 2 * 2 * NODES * FEATURES * FEATURES
+
+
+def tile_scalarproductattentiont_pa_kernel(tc, nodes, W, out):
+    nc = tc.nc
+    node_rows = nodes.flatten_outer_dims()
+    out_rows = out.flatten_outer_dims()
+
+    with ExitStack() as ctx:
+        keep = ctx.enter_context(tc.tile_pool(name="keep", bufs=1))
+        xpool = ctx.enter_context(tc.tile_pool(name="xpool", bufs=LOOKAHEAD + 2))
+        soft = ctx.enter_context(tc.tile_pool(name="soft", bufs=3))
+        banks = ctx.enter_context(tc.psum_pool(name="banks", bufs=8))
+
+        w_raw = keep.tile([P, PASSES, PACK, FEATURES], BF16)
+        for c in range(PASSES):
+            pass_rows = W[K_PASS * c : K_PASS * (c + 1), :]
+            nc.sync.dma_start(
+                out=w_raw[:, c, :, :].rearrange("p (u e) g -> p u e g", e=2),
+                in_=pass_rows.rearrange("(u p e) g -> p u e g", u=2, e=2),
+            )
+        n_raw = keep.tile([P, BLOCKS * FEATURES], BF16)
+        for b in range(BLOCKS):
+            nc.sync.dma_start(
+                out=n_raw[:, FEATURES * b : FEATURES * (b + 1)],
+                in_=node_rows[P * b : P * (b + 1), :],
+            )
+
+        ident = keep.tile([P, P], F32)
+        make_identity(nc, ident[:])
+
+        warm_in = keep.tile([P, 1], F32)
+        warm_out = keep.tile([P, 1], F32)
+        nc.vector.memset(warm_in[:], 0.0)
+        nc.scalar.activation(out=warm_out[:], in_=warm_in[:], func=ACT.Exp)
+
+        w_grouped = keep.tile([P, PASSES, FEATURES * PACK], BF16, align_bytes=64)
+        w_codes = keep.tile([P, PASSES, FEATURES], U32, align_bytes=64)
+        w_scales = keep.tile([P, PASSES, FEATURES], U8, align_bytes=64)
+        for c in range(PASSES):
+            for a in range(4):
+                dst = w_grouped[:, c, 1024 * a : 1024 * (a + 1)].rearrange(
+                    "p (e q t) -> p e q t", e=2, t=PACK
+                )
+                src = w_raw[:, c, :, 256 * a : 256 * (a + 1)].rearrange(
+                    "p t (q e) -> p e q t", e=2
+                )
+                if a == 3:
+                    nc.scalar.copy(out=dst, in_=src)
+                else:
+                    nc.vector.tensor_copy(out=dst, in_=src)
+            nc.vector.quantize_mx(
+                out=w_codes[:, c, :].bitcast(FP8X4),
+                scales=w_scales[:, c, :],
+                in_=w_grouped[:, c, :],
+            )
+
+        n_words = n_raw[:].bitcast(F32)
+        n_grouped = keep.tile([P, PASSES * NODES * PACK], BF16, align_bytes=64)
+        n_grouped_words = n_grouped[:].bitcast(F32).rearrange(
+            "p (c n u) -> p c n u", c=PASSES, u=2
+        )
+        n_codes = keep.tile([P, PASSES, NODES], U32, align_bytes=64)
+        n_scales = keep.tile([P, PASSES, NODES], U8, align_bytes=64)
+        for b in range(BLOCKS):
+            flipped = banks.tile([P, PASSES, 2, P], F32, tag="bank")
+            for c in range(PASSES):
+                for u in range(2):
+                    first_word = 512 * b + 256 * c + P * u
+                    nc.tensor.transpose(
+                        flipped[:, c, u, :], n_words[:, first_word : first_word + P], ident[:]
+                    )
+            nc.scalar.copy(
+                out=n_grouped_words[:, :, P * b : P * (b + 1), :],
+                in_=flipped[:].rearrange("p c u n -> p c n u"),
+            )
+            if b % 2 == 1:
+                first_node = P * (b - 1)
+                for c in range(PASSES):
+                    start = PACK * (NODES * c + first_node)
+                    nc.vector.quantize_mx(
+                        out=n_codes[:, c, first_node : first_node + 2 * P].bitcast(FP8X4),
+                        scales=n_scales[:, c, first_node : first_node + 2 * P],
+                        in_=n_grouped[:, start : start + 2 * P * PACK],
+                    )
+
+        def first_matmul(b):
+            x_grouped = xpool.tile([P, PASSES, P, PACK], BF16, align_bytes=64)
+            for co in range(PASSES):
+                xt = banks.tile([P, PACK, P], F32, tag="bank")
+                for t in range(PACK):
+                    j = PACK * co + t
+                    for c in range(PASSES):
+                        nc.tensor.matmul_mx(
+                            out=xt[:, t, :],
+                            lhsT=w_codes[:, c, P * j : P * (j + 1)].bitcast(FP8X4),
+                            lhsT_scale=w_scales[:, c, P * j : P * (j + 1)],
+                            rhs=n_codes[:, c, P * b : P * (b + 1)].bitcast(FP8X4),
+                            rhs_scale=n_scales[:, c, P * b : P * (b + 1)],
+                            start=(c == 0),
+                            stop=(c == PASSES - 1),
+                        )
+                if co == 0:
+                    nc.vector.tensor_copy(
+                        out=x_grouped[:, co, :, :], in_=xt[:].rearrange("p t n -> p n t")
+                    )
+                else:
+                    nc.scalar.copy(
+                        out=x_grouped[:, co, :, :], in_=xt[:].rearrange("p t n -> p n t")
+                    )
+            x_codes = xpool.tile([P, PASSES, P], U32, align_bytes=64)
+            x_scales = xpool.tile([P, PASSES, P], U8, align_bytes=64)
+            nc.vector.quantize_mx(
+                out=x_codes[:].rearrange("p c n -> p (c n)").bitcast(FP8X4),
+                scales=x_scales[:].rearrange("p c n -> p (c n)"),
+                in_=x_grouped[:].rearrange("p c n t -> p (c n t)"),
+            )
+            return x_codes, x_scales
+
+        def second_matmul_and_softmax(b, x_codes, x_scales):
+            prods = []
+            row_max = soft.tile([P, HALVES], F32)
+            for h in range(HALVES):
+                prod = banks.tile([P, BANK], F32, tag="bank")
+                for c in range(PASSES):
+                    nc.tensor.matmul_mx(
+                        out=prod[:],
+                        lhsT=x_codes[:, c, :].bitcast(FP8X4),
+                        lhsT_scale=x_scales[:, c, :],
+                        rhs=n_codes[:, c, BANK * h : BANK * (h + 1)].bitcast(FP8X4),
+                        rhs_scale=n_scales[:, c, BANK * h : BANK * (h + 1)],
+                        start=(c == 0),
+                        stop=(c == PASSES - 1),
+                    )
+                nc.vector.tensor_reduce(
+                    out=row_max[:, h : h + 1], in_=prod[:], axis=AXIS.X, op=ALU.max
+                )
+                prods.append(prod)
+            shift = soft.tile([P, 1], F32)
+            nc.vector.tensor_scalar(
+                out=shift[:],
+                in0=row_max[:, 0:1],
+                scalar1=row_max[:, 1:2],
+                scalar2=-1.0 / 32.0,
+                op0=ALU.max,
+                op1=ALU.mult,
+            )
+            expd = soft.tile([P, NODES], F32)
+            part_sum = soft.tile([P, HALVES], F32)
+            for h in range(HALVES):
+                nc.scalar.activation(
+                    out=expd[:, BANK * h : BANK * (h + 1)],
+                    in_=prods[h][:],
+                    func=ACT.Exp,
+                    bias=shift[:, 0:1],
+                    scale=1.0 / 32.0,
+                    accum_out=part_sum[:, h : h + 1],
+                )
+            row_sum = soft.tile([P, 1], F32)
+            nc.vector.tensor_reduce(out=row_sum[:], in_=part_sum[:], axis=AXIS.X, op=ALU.add)
+            inv_sum = soft.tile([P, 1], F32)
+            nc.vector.reciprocal(out=inv_sum[:], in_=row_sum[:])
+            weights = soft.tile([P, NODES], F32)
+            nc.vector.tensor_scalar(
+                out=weights[:], in0=expd[:], scalar1=inv_sum[:, 0:1], scalar2=None, op0=ALU.mult
+            )
+            nc.sync.dma_start(out=out_rows[P * b : P * (b + 1), :], in_=weights[:])
+
+        x_ready = []
+        for b in range(LOOKAHEAD):
+            x_ready.append(first_matmul(b))
+        for b in range(BLOCKS):
+            if b + LOOKAHEAD < BLOCKS:
+                x_ready.append(first_matmul(b + LOOKAHEAD))
+            x_codes, x_scales = x_ready[b]
+            second_matmul_and_softmax(b, x_codes, x_scales)

@@ -59,26 +59,24 @@ def tile_scalarproductattentiont_pa_kernel(tc, nodes, W, out):
         nc.vector.memset(warm_in[:], 0.0)
         nc.scalar.activation(out=warm_out[:], in_=warm_in[:], func=ACT.Exp)
 
-        w_grouped = keep.tile([P, PASSES, FEATURES * PACK], BF16, align_bytes=64)
-        w_codes = keep.tile([P, PASSES, FEATURES], U32, align_bytes=64)
-        w_scales = keep.tile([P, PASSES, FEATURES], U8, align_bytes=64)
+        w_grouped = keep.tile([P, PASSES, 2, BANK * PACK], BF16, align_bytes=64)
+        w_codes = keep.tile([P, PASSES, 2, BANK], U32, align_bytes=64)
+        w_scales = keep.tile([P, PASSES, 2, BANK], U8, align_bytes=64)
         for c in range(PASSES):
-            for a in range(4):
-                dst = w_grouped[:, c, 1024 * a : 1024 * (a + 1)].rearrange(
-                    "p (e q t) -> p e q t", e=2, t=PACK
-                )
-                src = w_raw[:, c, :, 256 * a : 256 * (a + 1)].rearrange(
-                    "p t (q e) -> p e q t", e=2
-                )
-                if a == 3:
-                    nc.scalar.copy(out=dst, in_=src)
+            for eo in range(2):
+                dst = w_grouped[:, c, eo, :].rearrange("p (r i t) -> p r t i", i=4, t=PACK)
+                src = w_raw[:, c, :, :].rearrange("p t (r i e) -> p e r t i", i=4, e=2)[:, eo]
+                nc.vector.tensor_copy(out=dst[:, 0:64], in_=src[:, 0:64])
+                if eo == 0:
+                    nc.vector.tensor_copy(out=dst[:, 64:128], in_=src[:, 64:128])
                 else:
-                    nc.vector.tensor_copy(out=dst, in_=src)
-            nc.vector.quantize_mx(
-                out=w_codes[:, c, :].bitcast(FP8X4),
-                scales=w_scales[:, c, :],
-                in_=w_grouped[:, c, :],
-            )
+                    nc.scalar.copy(out=dst[:, 64:128], in_=src[:, 64:128])
+            for eo in range(2):
+                nc.vector.quantize_mx(
+                    out=w_codes[:, c, eo, :].bitcast(FP8X4),
+                    scales=w_scales[:, c, eo, :],
+                    in_=w_grouped[:, c, eo, :],
+                )
 
         n_words = n_raw[:].bitcast(F32)
         n_grouped = keep.tile([P, PASSES * NODES * PACK], BF16, align_bytes=64)
@@ -114,12 +112,13 @@ def tile_scalarproductattentiont_pa_kernel(tc, nodes, W, out):
             for co in range(PASSES):
                 xt = banks.tile([P, PACK, P], F32, tag="bank")
                 for t in range(PACK):
-                    j = PACK * co + t
+                    eo = t % 2
+                    first = P * (2 * co + t // 2)
                     for c in range(PASSES):
                         nc.tensor.matmul_mx(
                             out=xt[:, t, :],
-                            lhsT=w_codes[:, c, P * j : P * (j + 1)].bitcast(FP8X4),
-                            lhsT_scale=w_scales[:, c, P * j : P * (j + 1)],
+                            lhsT=w_codes[:, c, eo, first : first + P].bitcast(FP8X4),
+                            lhsT_scale=w_scales[:, c, eo, first : first + P],
                             rhs=n_codes[:, c, P * b : P * (b + 1)].bitcast(FP8X4),
                             rhs_scale=n_scales[:, c, P * b : P * (b + 1)],
                             start=(c == 0),
@@ -186,10 +185,17 @@ def tile_scalarproductattentiont_pa_kernel(tc, nodes, W, out):
             inv_sum = soft.tile([P, 1], F32)
             nc.vector.reciprocal(out=inv_sum[:], in_=row_sum[:])
             weights = soft.tile([P, NODES], F32)
-            nc.vector.tensor_scalar(
-                out=weights[:], in0=expd[:], scalar1=inv_sum[:, 0:1], scalar2=None, op0=ALU.mult
-            )
-            nc.sync.dma_start(out=out_rows[P * b : P * (b + 1), :], in_=weights[:])
+            for h in range(HALVES):
+                cols = slice(BANK * h, BANK * (h + 1))
+                nc.gpsimd.tensor_scalar(
+                    out=weights[:, cols],
+                    in0=expd[:, cols],
+                    scalar1=inv_sum[:, 0:1],
+                    scalar2=0.0,
+                    op0=ALU.mult,
+                    op1=ALU.add,
+                )
+                nc.sync.dma_start(out=out_rows[P * b : P * (b + 1), cols], in_=weights[:, cols])
 
         x_ready = []
         for b in range(LOOKAHEAD):

@@ -14,6 +14,7 @@ AXIS = mybir.AxisListType
 
 P = 128
 PACK = 4
+PAIR = 2
 K_PASS = P * PACK
 NODES = 1024
 FEATURES = 1024
@@ -21,7 +22,10 @@ PASSES = FEATURES // K_PASS
 BLOCKS = NODES // P
 BANK = 512
 HALVES = NODES // BANK
+RUN = 4
+RUNS = FEATURES // PAIR // RUN
 LOOKAHEAD = 2
+SCALE = 1.0 / 32.0
 
 FLOPS = 2 * 2 * NODES * FEATURES * FEATURES
 
@@ -41,8 +45,8 @@ def tile_scalarproductattentiont_pa_kernel(tc, nodes, W, out):
         for c in range(PASSES):
             pass_rows = W[K_PASS * c : K_PASS * (c + 1), :]
             nc.sync.dma_start(
-                out=w_raw[:, c, :, :].rearrange("p (u e) g -> p u e g", e=2),
-                in_=pass_rows.rearrange("(u p e) g -> p u e g", u=2, e=2),
+                out=w_raw[:, c, :, :].rearrange("p (u e) g -> p u e g", e=PAIR),
+                in_=pass_rows.rearrange("(u p e) g -> p u e g", u=PAIR, e=PAIR),
             )
         n_raw = keep.tile([P, BLOCKS * FEATURES], BF16)
         for b in range(BLOCKS):
@@ -59,19 +63,21 @@ def tile_scalarproductattentiont_pa_kernel(tc, nodes, W, out):
         nc.vector.memset(warm_in[:], 0.0)
         nc.scalar.activation(out=warm_out[:], in_=warm_in[:], func=ACT.Exp)
 
-        w_grouped = keep.tile([P, PASSES, 2, BANK * PACK], BF16, align_bytes=64)
-        w_codes = keep.tile([P, PASSES, 2, BANK], U32, align_bytes=64)
-        w_scales = keep.tile([P, PASSES, 2, BANK], U8, align_bytes=64)
+        w_grouped = keep.tile([P, PASSES, PAIR, BANK * PACK], BF16, align_bytes=64)
+        w_codes = keep.tile([P, PASSES, PAIR, BANK], U32, align_bytes=64)
+        w_scales = keep.tile([P, PASSES, PAIR, BANK], U8, align_bytes=64)
         for c in range(PASSES):
-            for eo in range(2):
-                dst = w_grouped[:, c, eo, :].rearrange("p (r i t) -> p r t i", i=4, t=PACK)
-                src = w_raw[:, c, :, :].rearrange("p t (r i e) -> p e r t i", i=4, e=2)[:, eo]
-                nc.vector.tensor_copy(out=dst[:, 0:64], in_=src[:, 0:64])
+            for eo in range(PAIR):
+                dst = w_grouped[:, c, eo, :].rearrange("p (r i t) -> p r t i", i=RUN, t=PACK)
+                src = w_raw[:, c, :, :].rearrange("p t (r i e) -> p e r t i", i=RUN, e=PAIR)[:, eo]
+                first_half = slice(0, RUNS // 2)
+                second_half = slice(RUNS // 2, RUNS)
+                nc.vector.tensor_copy(out=dst[:, first_half], in_=src[:, first_half])
                 if eo == 0:
-                    nc.vector.tensor_copy(out=dst[:, 64:128], in_=src[:, 64:128])
+                    nc.vector.tensor_copy(out=dst[:, second_half], in_=src[:, second_half])
                 else:
-                    nc.scalar.copy(out=dst[:, 64:128], in_=src[:, 64:128])
-            for eo in range(2):
+                    nc.scalar.copy(out=dst[:, second_half], in_=src[:, second_half])
+            for eo in range(PAIR):
                 nc.vector.quantize_mx(
                     out=w_codes[:, c, eo, :].bitcast(FP8X4),
                     scales=w_scales[:, c, eo, :],
@@ -81,15 +87,15 @@ def tile_scalarproductattentiont_pa_kernel(tc, nodes, W, out):
         n_words = n_raw[:].bitcast(F32)
         n_grouped = keep.tile([P, PASSES * NODES * PACK], BF16, align_bytes=64)
         n_grouped_words = n_grouped[:].bitcast(F32).rearrange(
-            "p (c n u) -> p c n u", c=PASSES, u=2
+            "p (c n u) -> p c n u", c=PASSES, u=PAIR
         )
         n_codes = keep.tile([P, PASSES, NODES], U32, align_bytes=64)
         n_scales = keep.tile([P, PASSES, NODES], U8, align_bytes=64)
         for b in range(BLOCKS):
-            flipped = banks.tile([P, PASSES, 2, P], F32, tag="bank")
+            flipped = banks.tile([P, PASSES, PAIR, P], F32, tag="bank")
             for c in range(PASSES):
-                for u in range(2):
-                    first_word = 512 * b + 256 * c + P * u
+                for u in range(PAIR):
+                    first_word = ((b * PASSES + c) * PAIR + u) * P
                     nc.tensor.transpose(
                         flipped[:, c, u, :], n_words[:, first_word : first_word + P], ident[:]
                     )
@@ -112,8 +118,8 @@ def tile_scalarproductattentiont_pa_kernel(tc, nodes, W, out):
             for co in range(PASSES):
                 xt = banks.tile([P, PACK, P], F32, tag="bank")
                 for t in range(PACK):
-                    eo = t % 2
-                    first = P * (2 * co + t // 2)
+                    eo = t % PAIR
+                    first = P * (PAIR * co + t // PAIR)
                     for c in range(PASSES):
                         nc.tensor.matmul_mx(
                             out=xt[:, t, :],
@@ -165,7 +171,7 @@ def tile_scalarproductattentiont_pa_kernel(tc, nodes, W, out):
                 out=shift[:],
                 in0=row_max[:, 0:1],
                 scalar1=row_max[:, 1:2],
-                scalar2=-1.0 / 32.0,
+                scalar2=-SCALE,
                 op0=ALU.max,
                 op1=ALU.mult,
             )
@@ -177,17 +183,18 @@ def tile_scalarproductattentiont_pa_kernel(tc, nodes, W, out):
                     in_=prods[h][:],
                     func=ACT.Exp,
                     bias=shift[:, 0:1],
-                    scale=1.0 / 32.0,
+                    scale=SCALE,
                     accum_out=part_sum[:, h : h + 1],
                 )
             row_sum = soft.tile([P, 1], F32)
             nc.vector.tensor_reduce(out=row_sum[:], in_=part_sum[:], axis=AXIS.X, op=ALU.add)
             inv_sum = soft.tile([P, 1], F32)
             nc.vector.reciprocal(out=inv_sum[:], in_=row_sum[:])
+            normaliser = nc.vector if b == BLOCKS - 1 else nc.gpsimd
             weights = soft.tile([P, NODES], F32)
             for h in range(HALVES):
                 cols = slice(BANK * h, BANK * (h + 1))
-                nc.gpsimd.tensor_scalar(
+                normaliser.tensor_scalar(
                     out=weights[:, cols],
                     in0=expd[:, cols],
                     scalar1=inv_sum[:, 0:1],

from contextlib import ExitStack

import concourse.mybir as mybir
from concourse.masks import make_identity

BF16 = mybir.dt.bfloat16
F32 = mybir.dt.float32
U32 = mybir.dt.uint32
U8 = mybir.dt.uint8
FP8X4 = mybir.dt.float8_e4m3fn_x4
ACT = mybir.ActivationFunctionType
ALU = mybir.AluOpType
AXIS = mybir.AxisListType

P = 128
PACK = 4
PAIR = 2
K_PASS = P * PACK
NODES = 1024
FEATURES = 1024
PASSES = FEATURES // K_PASS
BLOCKS = NODES // P
BANK = 512
HALVES = NODES // BANK
RUN = 4
RUNS = FEATURES // PAIR // RUN
LOOKAHEAD = 2
SCALE = 1.0 / 32.0

FLOPS = 2 * 2 * NODES * FEATURES * FEATURES


def tile_scalarproductattentiont_pa_kernel(tc, nodes, W, out):
    nc = tc.nc
    node_rows = nodes.flatten_outer_dims()
    out_rows = out.flatten_outer_dims()

    with ExitStack() as ctx:
        keep = ctx.enter_context(tc.tile_pool(name="keep", bufs=1))
        xpool = ctx.enter_context(tc.tile_pool(name="xpool", bufs=LOOKAHEAD + 2))
        soft = ctx.enter_context(tc.tile_pool(name="soft", bufs=3))
        banks = ctx.enter_context(tc.psum_pool(name="banks", bufs=8))

        w_raw = keep.tile([P, PASSES, PACK, FEATURES], BF16)
        for c in range(PASSES):
            pass_rows = W[K_PASS * c : K_PASS * (c + 1), :]
            nc.sync.dma_start(
                out=w_raw[:, c, :, :].rearrange("p (u e) g -> p u e g", e=PAIR),
                in_=pass_rows.rearrange("(u p e) g -> p u e g", u=PAIR, e=PAIR),
            )
        n_raw = keep.tile([P, BLOCKS * FEATURES], BF16)
        for b in range(BLOCKS):
            nc.sync.dma_start(
                out=n_raw[:, FEATURES * b : FEATURES * (b + 1)],
                in_=node_rows[P * b : P * (b + 1), :],
            )

        ident = keep.tile([P, P], F32)
        make_identity(nc, ident[:])

        warm_in = keep.tile([P, 1], F32)
        warm_out = keep.tile([P, 1], F32)
        nc.vector.memset(warm_in[:], 0.0)
        nc.scalar.activation(out=warm_out[:], in_=warm_in[:], func=ACT.Exp)

        w_grouped = keep.tile([P, PASSES, PAIR, BANK * PACK], BF16, align_bytes=64)
        w_codes = keep.tile([P, PASSES, PAIR, BANK], U32, align_bytes=64)
        w_scales = keep.tile([P, PASSES, PAIR, BANK], U8, align_bytes=64)
        for c in range(PASSES):
            for eo in range(PAIR):
                dst = w_grouped[:, c, eo, :].rearrange("p (r i t) -> p r t i", i=RUN, t=PACK)
                src = w_raw[:, c, :, :].rearrange("p t (r i e) -> p e r t i", i=RUN, e=PAIR)[:, eo]
                first_half = slice(0, RUNS // 2)
                second_half = slice(RUNS // 2, RUNS)
                nc.vector.tensor_copy(out=dst[:, first_half], in_=src[:, first_half])
                if eo == 0:
                    nc.vector.tensor_copy(out=dst[:, second_half], in_=src[:, second_half])
                else:
                    nc.scalar.copy(out=dst[:, second_half], in_=src[:, second_half])
            for eo in range(PAIR):
                nc.vector.quantize_mx(
                    out=w_codes[:, c, eo, :].bitcast(FP8X4),
                    scales=w_scales[:, c, eo, :],
                    in_=w_grouped[:, c, eo, :],
                )

        n_words = n_raw[:].bitcast(F32)
        n_grouped = keep.tile([P, PASSES * NODES * PACK], BF16, align_bytes=64)
        n_grouped_words = n_grouped[:].bitcast(F32).rearrange(
            "p (c n u) -> p c n u", c=PASSES, u=PAIR
        )
        n_codes = keep.tile([P, PASSES, NODES], U32, align_bytes=64)
        n_scales = keep.tile([P, PASSES, NODES], U8, align_bytes=64)
        for b in range(BLOCKS):
            flipped = banks.tile([P, PASSES, PAIR, P], F32, tag="bank")
            for c in range(PASSES):
                for u in range(PAIR):
                    first_word = ((b * PASSES + c) * PAIR + u) * P
                    nc.tensor.transpose(
                        flipped[:, c, u, :], n_words[:, first_word : first_word + P], ident[:]
                    )
            nc.scalar.copy(
                out=n_grouped_words[:, :, P * b : P * (b + 1), :],
                in_=flipped[:].rearrange("p c u n -> p c n u"),
            )
            if b % 2 == 1:
                first_node = P * (b - 1)
                for c in range(PASSES):
                    start = PACK * (NODES * c + first_node)
                    nc.vector.quantize_mx(
                        out=n_codes[:, c, first_node : first_node + 2 * P].bitcast(FP8X4),
                        scales=n_scales[:, c, first_node : first_node + 2 * P],
                        in_=n_grouped[:, start : start + 2 * P * PACK],
                    )

        def first_matmul(b):
            x_grouped = xpool.tile([P, PASSES, P, PACK], BF16, align_bytes=64)
            for co in range(PASSES):
                xt = banks.tile([P, PACK, P], F32, tag="bank")
                for t in range(PACK):
                    eo = t % PAIR
                    first = P * (PAIR * co + t // PAIR)
                    for c in range(PASSES):
                        nc.tensor.matmul_mx(
                            out=xt[:, t, :],
                            lhsT=w_codes[:, c, eo, first : first + P].bitcast(FP8X4),
                            lhsT_scale=w_scales[:, c, eo, first : first + P],
                            rhs=n_codes[:, c, P * b : P * (b + 1)].bitcast(FP8X4),
                            rhs_scale=n_scales[:, c, P * b : P * (b + 1)],
                            start=(c == 0),
                            stop=(c == PASSES - 1),
                        )
                if co == 0:
                    nc.vector.tensor_copy(
                        out=x_grouped[:, co, :, :], in_=xt[:].rearrange("p t n -> p n t")
                    )
                else:
                    nc.scalar.copy(
                        out=x_grouped[:, co, :, :], in_=xt[:].rearrange("p t n -> p n t")
                    )
            x_codes = xpool.tile([P, PASSES, P], U32, align_bytes=64)
            x_scales = xpool.tile([P, PASSES, P], U8, align_bytes=64)
            nc.vector.quantize_mx(
                out=x_codes[:].rearrange("p c n -> p (c n)").bitcast(FP8X4),
                scales=x_scales[:].rearrange("p c n -> p (c n)"),
                in_=x_grouped[:].rearrange("p c n t -> p (c n t)"),
            )
            return x_codes, x_scales

        def second_matmul_and_softmax(b, x_codes, x_scales):
            prods = []
            row_max = soft.tile([P, HALVES], F32)
            for h in range(HALVES):
                prod = banks.tile([P, BANK], F32, tag="bank")
                for c in range(PASSES):
                    nc.tensor.matmul_mx(
                        out=prod[:],
                        lhsT=x_codes[:, c, :].bitcast(FP8X4),
                        lhsT_scale=x_scales[:, c, :],
                        rhs=n_codes[:, c, BANK * h : BANK * (h + 1)].bitcast(FP8X4),
                        rhs_scale=n_scales[:, c, BANK * h : BANK * (h + 1)],
                        start=(c == 0),
                        stop=(c == PASSES - 1),
                    )
                nc.vector.tensor_reduce(
                    out=row_max[:, h : h + 1], in_=prod[:], axis=AXIS.X, op=ALU.max
                )
                prods.append(prod)
            shift = soft.tile([P, 1], F32)
            nc.vector.tensor_scalar(
                out=shift[:],
                in0=row_max[:, 0:1],
                scalar1=row_max[:, 1:2],
                scalar2=-SCALE,
                op0=ALU.max,
                op1=ALU.mult,
            )
            expd = soft.tile([P, NODES], F32)
            part_sum = soft.tile([P, HALVES], F32)
            for h in range(HALVES):
                nc.scalar.activation(
                    out=expd[:, BANK * h : BANK * (h + 1)],
                    in_=prods[h][:],
                    func=ACT.Exp,
                    bias=shift[:, 0:1],
                    scale=SCALE,
                    accum_out=part_sum[:, h : h + 1],
                )
            row_sum = soft.tile([P, 1], F32)
            nc.vector.tensor_reduce(out=row_sum[:], in_=part_sum[:], axis=AXIS.X, op=ALU.add)
            inv_sum = soft.tile([P, 1], F32)
            nc.vector.reciprocal(out=inv_sum[:], in_=row_sum[:])
            normaliser = nc.vector if b == BLOCKS - 1 else nc.gpsimd
            weights = soft.tile([P, NODES], F32)
            for h in range(HALVES):
                cols = slice(BANK * h, BANK * (h + 1))
                normaliser.tensor_scalar(
                    out=weights[:, cols],
                    in0=expd[:, cols],
                    scalar1=inv_sum[:, 0:1],
                    scalar2=0.0,
                    op0=ALU.mult,
                    op1=ALU.add,
                )
                nc.sync.dma_start(out=out_rows[P * b : P * (b + 1), cols], in_=weights[:, cols])

        x_ready = []
        for b in range(LOOKAHEAD):
            x_ready.append(first_matmul(b))
        for b in range(BLOCKS):
            if b + LOOKAHEAD < BLOCKS:
                x_ready.append(first_matmul(b + LOOKAHEAD))
            x_codes, x_scales = x_ready[b]
            second_matmul_and_softmax(b, x_codes, x_scales)
